import numpy as np
import ml_dtypes


def mxq(x, axis, fmt="e4m3"):
    dtype, down = {"e4m3": (ml_dtypes.float8_e4m3fn, 7), "e5m2": (ml_dtypes.float8_e5m2, 14)}[fmt]
    v = np.moveaxis(np.asarray(x, np.float32).astype(ml_dtypes.bfloat16).astype(np.float64), axis, -1)
    blocks = v.reshape(v.shape[:-1] + (-1, 32))
    amax = np.abs(blocks).max(-1, keepdims=True)
    byte = np.maximum(np.where(amax > 0, np.frexp(amax)[1] - 1 + 127, 0) - down, 1)
    scale = np.exp2(byte - 127.0)
    codes = (blocks / scale).astype(np.float32).astype(dtype).astype(np.float64)
    return np.moveaxis((codes * scale).reshape(v.shape), -1, axis)


WIDE = False


def mx_kscale(k):
    if not WIDE:
        return np.ones(k)
    levels = np.array([10, -10, 5, -5, 0])
    if k % 512:
        return np.exp2(np.random.permutation(np.resize(levels, k // 32))).repeat(32)
    a = np.empty((k // 512, 16))
    for p in range(k // 512):
        a[p, :8] = np.random.permutation(np.resize(levels, 8))
        for g in range(8):
            far = levels[np.abs(levels - a[p, g]) >= 10]
            a[p, g + 8] = far[np.random.randint(len(far))]
    return np.exp2(a.ravel()).repeat(32)


BF16 = ml_dtypes.bfloat16


def bf(x):
    return np.asarray(x, np.float32).astype(BF16)


def f64(x):
    return np.asarray(x).astype(np.float64)


BQ, BK, L, H, DH = 64, 4, 128, 4, 128
D = H * DH


def draw0():
    s, t = mx_kscale(D), mx_kscale(D)
    amp_q = 0.5 + np.random.random((BQ, 1, 1))
    amp_k = 0.5 + np.random.random((BK, 1, 1))
    return {
        "query_states": bf(np.random.standard_normal((BQ, L, D)) * amp_q * s),
        "key_states": bf(np.random.standard_normal((BK, L, D)) * amp_k * s),
        "Wq": bf(np.random.standard_normal((D, D)) * 0.8 / np.sqrt(D) * t[:, None] / s[None, :]),
        "bq": bf(np.random.standard_normal(D) * 0.3 * t),
        "Wk": bf(np.random.standard_normal((D, D)) * 0.8 / np.sqrt(D) / t[:, None] / s[None, :]),
        "bk": bf(np.random.standard_normal(D) * 0.3 / t),
        "logit_scale": bf(-1.5 + 0.1 * np.random.standard_normal(1)),
    }


def core(query_states, key_states, Wq, bq, Wk, bk, logit_scale):
    q = (mxq(f64(query_states).reshape(BQ * L, D), 1, "e4m3") @ mxq(f64(Wq), 1, "e4m3").T) + f64(bq)
    k = (mxq(f64(key_states).reshape(BK * L, D), 1, "e4m3") @ mxq(f64(Wk), 1, "e4m3").T) + f64(bk)
    retrieve = mxq(q, 1, "e4m3") @ mxq(k, 1, "e4m3").T
    retrieve = retrieve.reshape(BQ, L, BK, L).transpose(0, 2, 1, 3)
    t2v = retrieve.max(axis=-1).sum(axis=2) / L
    v2t = retrieve.max(axis=-2).sum(axis=2) / L
    return np.exp(f64(logit_scale)) * (t2v + v2t) / 2.0


def e4m3fn_bytes(y):
    return np.clip(np.asarray(y, np.float64), -448.0, 448.0).astype(np.float32).astype(ml_dtypes.float8_e4m3fn).view(np.uint8)


def e4m3fn_values(b):
    return np.asarray(b, np.uint8).view(ml_dtypes.float8_e4m3fn).astype(np.float64)


def setup_inputs():
    d = draw0()
    x0 = np.asarray(d['query_states']).astype(np.float64)
    s = (np.max(np.abs(x0), axis=(0, 1), keepdims=True) / 448.0).astype(np.float32)
    out = {}
    for k, v in d.items():
        if k == 'query_states':
            out['query_states_bytes'] = e4m3fn_bytes(x0 / s.astype(np.float64))
            out['query_states_scale'] = s
        else:
            out[k] = v
    return out


def reference(query_states_bytes, query_states_scale, key_states, Wq, bq, Wk, bk, logit_scale):
    return core(e4m3fn_values(query_states_bytes) * query_states_scale.astype(np.float64), key_states, Wq, bq, Wk, bk, logit_scale)

from contextlib import ExitStack

import concourse.mybir as mybir
from concourse.masks import make_identity

F32 = mybir.dt.float32
BF16 = mybir.dt.bfloat16
U32 = mybir.dt.uint32
U8 = mybir.dt.uint8
FP8 = mybir.dt.float8_e4m3fn
FP8X4 = mybir.dt.float8_e4m3fn_x4
ALU = mybir.AluOpType
ACT = mybir.ActivationFunctionType
AX = mybir.AxisListType

P = 128
D = 512
GT = 4
NG = 16
FLOPS = 2 * 8192 * 512 * 512 * 2 + 2 * 512 * 512 * 512

def on_vector(g, c):
    return g < 2 or c == 0

S_COLS = 224


def tile_attention_pa_t_kernel(tc, xb_d, xs_d, key_d, wq_d, bq_d, wk_d, bk_d, ls_d, out_d):
    nc = tc.nc
    with ExitStack() as ctx:
        keep = ctx.enter_context(tc.tile_pool(name="keep", bufs=1))
        work = ctx.enter_context(tc.tile_pool(name="work", bufs=3))
        psq = ctx.enter_context(tc.psum_pool(name="psq", bufs=1))
        psr = ctx.enter_context(tc.psum_pool(name="psr", bufs=2))
        pst = ctx.enter_context(tc.psum_pool(name="pst", bufs=2))
        ctx.enter_context(tc.manual_schedule())

        ident = keep.tile([P, P], F32, name="ident")
        ones = keep.tile([P, P], F32, name="ones")
        warm = keep.tile([P, 1], F32, name="warm")
        wk_raw = keep.tile([P, 4, D], BF16, name="wk_raw", align_bytes=64)
        wq_raw = keep.tile([P, 4, D], BF16, name="wq_raw", align_bytes=64)
        key_raw = keep.tile([P, 4, D], BF16, name="key_raw", align_bytes=64)
        sc = keep.tile([P, D], F32, name="sc", align_bytes=64)
        bq = keep.tile([P, 4], BF16, name="bq")
        bk = keep.tile([P, 4], BF16, name="bk")
        ls = keep.tile([P, 1], BF16, name="ls")
        es = keep.tile([P, 1], F32, name="es")
        sel = keep.tile([P, 64], F32, name="sel")
        umax = keep.tile([P, D], F32, name="umax")
        tmax = keep.tile([P, 64, 4], F32, name="tmax")

        xv = xb_d.rearrange("a (h j) k -> (a h) j k", h=2)
        chunk_rows = [4, 4] + [8] * 7
        chunk_of = {}
        nc.sync.dma_start(out=wk_raw[:], in_=wk_d.rearrange("(m t) i -> m t i", t=4))
        nc.sync.dma_start(out=key_raw[:], in_=key_d.rearrange("b m k -> m b k"))
        nc.sync.dma_start(out=sc[:], in_=xs_d.rearrange("o u k -> (o u k)").partition_broadcast(P))
        j0 = 0
        for ci, nr in enumerate(chunk_rows):
            xb = keep.tile([P, nr, D], U8, name="xb" + str(ci), align_bytes=64)
            nc.sync.dma_start(out=xb[:], in_=xv[:, j0:j0 + nr, :])
            for r in range(nr):
                chunk_of[j0 + r] = (xb, r)
            j0 += nr
            if ci == 0:
                nc.sync.dma_start(out=wq_raw[:], in_=wq_d.rearrange("(m t) i -> m t i", t=4))
                nc.sync.dma_start(out=bk[:], in_=bk_d.rearrange("(p t) -> p t", t=4))
                nc.sync.dma_start(out=bq[:], in_=bq_d.rearrange("(p t) -> p t", t=4))
                nc.sync.dma_start(out=ls[:], in_=ls_d.partition_broadcast(P))

        nc.vector.memset(warm[:], 0.0)
        nc.scalar.activation(out=warm[:], in_=warm[:], func=ACT.Exp)
        make_identity(nc, ident[:])
        nc.vector.memset(ones[:], 1.0 / 256.0)
        nc.vector.tensor_tensor(out=sel[:], in0=ident[:, 0::2], in1=ident[:, 1::2], op=ALU.add)

        st = {}

        def codes_tile(name):
            c = work.tile([P, D], U32, name=name + "c", tag="codes", bufs=8, align_bytes=64)
            s = work.tile([P, D], U8, name=name + "s", tag="scales", bufs=8, align_bytes=64)
            return c, s

        def keep_codes(name):
            c = keep.tile([P, D], U32, name=name + "c", align_bytes=64)
            s = keep.tile([P, D], U8, name=name + "s", align_bytes=64)
            return c, s

        def quantize(dst, src):
            nc.vector.quantize_mx(out=dst[0][:].bitcast(FP8X4), scales=dst[1][:], in_=src[:].rearrange("p n t -> p (n t)"))

        def new_grouped(name):
            return work.tile([P, D, 4], BF16, name=name, tag="grouped", bufs=5, align_bytes=64)

        def turn(raw, grouped, half, copy):
            xt = pst.tile([P, 2, 2, P], F32, name="xt", tag="xt")
            words = raw[:].rearrange("p c k -> p (c k)").bitcast(F32)
            for i in range(2):
                w0 = 256 * (2 * half + i)
                for u in range(2):
                    nc.tensor.transpose(xt[:, i, u, :], words[:, w0 + u:w0 + 256:2], ident[:])
            dst = grouped[:].rearrange("p n t -> p (n t)").bitcast(F32)[:, 512 * half:512 * half + 512]
            copy(out=dst.rearrange("p (i r u) -> p i r u", i=2, u=2), in_=xt[:].rearrange("p i u r -> p i r u"))

        def mm(out, lhs, lcol, rhs, n):
            nc.tensor.matmul_mx(
                out=out,
                lhsT=lhs[0][:, lcol:lcol + P].bitcast(FP8X4),
                lhsT_scale=lhs[1][:, lcol:lcol + P],
                rhs=rhs[0][:, 0:n].bitcast(FP8X4),
                rhs_scale=rhs[1][:, 0:n],
                start=True,
                stop=True,
            )

        def project(name, w, x):
            tiles = []
            for t in range(4):
                q = psq.tile([P, D], F32, name="q" + str(t), tag="q" + str(t))
                mm(q[:], w, P * t, x, D)
                tiles.append(q)
            return tiles

        def add_bias(tiles, bias):
            pl = work.tile([P, 4, D], BF16, name="pl", tag="pl", bufs=2, align_bytes=64)
            for t in range(4):
                nc.scalar.activation(out=pl[:, t, :], in_=tiles[t][:], func=ACT.Identity, bias=bias[:, t:t + 1])
            return pl

        def weave(engine, grouped, pl, lo, hi):
            if hi <= lo:
                return
            dst = grouped[:, lo:hi, :]
            src = pl[:, :, lo:hi].rearrange("p t n -> p n t")
            if engine == "V":
                nc.vector.tensor_copy(out=dst, in_=src)
            elif engine == "S":
                nc.scalar.copy(out=dst, in_=src)
            else:
                nc.gpsimd.tensor_scalar(out=dst, in0=src, scalar1=1.0, scalar2=0.0, op0=ALU.mult, op1=ALU.add)

        xsg = {}
        wide = {}

        def rows_tile(g):
            if g not in xsg:
                xsg[g] = work.tile([P, 4, D], BF16, name="xsg", tag="xsg", bufs=5, align_bytes=64)
            return xsg[g]

        def codes_view(g, c):
            xb, r = chunk_of[4 * g + c]
            return xb[:, r, :].bitcast(FP8)

        def scale_v(g, c):
            nc.vector.tensor_tensor(out=rows_tile(g)[:, c, :], in0=codes_view(g, c), in1=sc[:], op=ALU.mult)

        def widen(g):
            if g >= NG:
                return
            for c in range(4):
                if not on_vector(g, c):
                    w = work.tile([P, D], BF16, name="xw", tag="xw", bufs=8, align_bytes=64)
                    nc.scalar.copy(out=w[:], in_=codes_view(g, c))
                    wide[(g, c)] = w

        def scale_g(g, cs):
            if g >= NG:
                return
            for c in cs:
                if not on_vector(g, c):
                    nc.gpsimd.tensor_tensor(out=rows_tile(g)[:, c, :], in0=wide[(g, c)][:], in1=sc[:], op=ALU.mult)

        def scale_vs(g):
            if g >= NG:
                return
            for c in range(4):
                if on_vector(g, c):
                    scale_v(g, c)

        rbank = {}

        def dots(g, c):
            if g >= NG:
                return
            r = psr.tile([P, D], F32, name="r", tag="r")
            mm(r[:], st[("q", g)], P * c, kcodes, D)
            rbank[(g, c)] = r

        def maxima(g, c):
            r = rbank[(g, c)]
            j = 4 * g + c
            def rowmax():
                nc.vector.tensor_reduce(out=tmax[:, j, :], in_=r[:].rearrange("p (b m) -> p b m", b=4), axis=AX.X, op=ALU.max)
            if j == 0:
                nc.scalar.copy(out=umax[:], in_=r[:])
                rowmax()
            elif j == 63:
                nc.vector.tensor_tensor(out=umax[:], in0=r[:], in1=umax[:], op=ALU.max)
                rowmax()
            else:
                rowmax()
                nc.vector.tensor_tensor(out=umax[:], in0=r[:], in1=umax[:], op=ALU.max)

        vcopy, scopy = nc.vector.tensor_copy, nc.scalar.copy
        wkc, wqc, keyc, kcodes = keep_codes("wk"), keep_codes("wq"), keep_codes("key"), keep_codes("k")
        g_wk, g_key = new_grouped("g_wk"), new_grouped("g_key")
        turn(wk_raw, g_wk, 0, scopy)
        turn(wk_raw, g_wk, 1, vcopy)
        quantize(wkc, g_wk)
        turn(key_raw, g_key, 0, scopy)
        turn(key_raw, g_key, 1, vcopy)
        scale_v(0, 0)
        quantize(keyc, g_key)
        kt = project("k", wkc, keyc)
        kpl = add_bias(kt, bk)
        for c in range(1, 4):
            scale_v(0, c)
        g_wq = new_grouped("g_wq")
        turn(wq_raw, g_wq, 0, scopy)
        turn(wq_raw, g_wq, 1, scopy)
        g_x = {}
        g_x[0] = new_grouped("g_x")
        turn(rows_tile(0), g_x[0], 0, vcopy)
        turn(rows_tile(0), g_x[0], 1, vcopy)
        quantize(wqc, g_wq)
        st[("x", 0)] = codes_tile("x")
        quantize(st[("x", 0)], g_x[0])
        qps = {}
        qps[0] = project("q", wqc, st[("x", 0)])
        pls = {}
        pls[0] = add_bias(qps[0], bq)
        scale_vs(1)
        widen(2)
        scale_g(2, range(4))
        g_k = new_grouped("g_k")
        weave("V", g_k, kpl, 0, D)
        scale_vs(2)
        quantize(kcodes, g_k)
        g_x[1] = new_grouped("g_x")
        turn(rows_tile(1), g_x[1], 0, scopy)
        turn(rows_tile(1), g_x[1], 1, vcopy)
        st[("x", 1)] = codes_tile("x")
        quantize(st[("x", 1)], g_x[1])
        qps[1] = project("q", wqc, st[("x", 1)])
        g_q = {}
        g_q[0] = new_grouped("g_q")
        weave("S", g_q[0], pls[0], 0, 256)
        weave("V", g_q[0], pls[0], 256, D)
        widen(3)
        scale_g(3, range(4))
        scale_vs(3)
        st[("q", 0)] = codes_tile("q")
        quantize(st[("q", 0)], g_q[0])
        dots(0, 0)
        g_x[2] = new_grouped("g_x")
        turn(rows_tile(2), g_x[2], 0, scopy)
        turn(rows_tile(2), g_x[2], 1, vcopy)
        widen(4)
        nc.scalar.activation(out=es[:], in_=ls[:], func=ACT.Exp)

        for i in range(NG):
            nxt = i + 1 < NG
            dots(i, 1)
            if nxt:
                pls[i + 1] = add_bias(qps[i + 1], bq)
            scale_g(i + 4, [0, 1])
            maxima(i, 0)
            if i + 2 < NG:
                st[("x", i + 2)] = codes_tile("x")
                quantize(st[("x", i + 2)], g_x[i + 2])
            dots(i, 2)
            if i + 2 < NG:
                qps[i + 2] = project("q", wqc, st[("x", i + 2)])
            if nxt:
                g_q[i + 1] = new_grouped("g_q")
                weave("S", g_q[i + 1], pls[i + 1], 0, S_COLS)
                weave("G", g_q[i + 1], pls[i + 1], S_COLS, D)
            maxima(i, 1)
            dots(i, 3)
            scale_vs(i + 4)
            if i + 3 < NG:
                g_x[i + 3] = new_grouped("g_x")
                turn(rows_tile(i + 3), g_x[i + 3], 0, scopy)
                turn(rows_tile(i + 3), g_x[i + 3], 1, scopy)
            maxima(i, 2)
            if nxt:
                st[("q", i + 1)] = codes_tile("q")
                quantize(st[("q", i + 1)], g_q[i + 1])
                dots(i + 1, 0)
            maxima(i, 3)
            widen(i + 5)
            scale_g(i + 4, [2, 3])

        ut = pst.tile([P, 4, P], F32, name="ut", tag="xt")
        for b in range(4):
            nc.tensor.transpose(ut[:, b, :], umax[:, P * b:P * b + P], ident[:])
        fin = pst.tile([P, 64, 4], F32, name="fin", tag="xt")
        tsum = keep.tile([P, 4], F32, name="tsum")
        z = keep.tile([P, 64, 4], F32, name="z")
        vm = keep.tile([P, 64, 4], F32, name="vm")
        row = keep.tile([P, 256], F32, name="row")
        nc.vector.tensor_reduce(out=tsum[:], in_=tmax[:].rearrange("p j b -> p b j"), axis=AX.X, op=ALU.add)
        nc.vector.tensor_reduce(out=vm[:], in_=ut[:].rearrange("p b (a h) -> p a b h", h=2), axis=AX.X, op=ALU.max)
        nc.vector.tensor_tensor(
            out=z[:],
            in0=sel[:].unsqueeze(2).to_broadcast([P, 64, 4]),
            in1=tsum[:].unsqueeze(1).to_broadcast([P, 64, 4]),
            op=ALU.mult,
        )
        finf = fin[:].rearrange("p a b -> p (a b)")
        nc.tensor.matmul(finf, lhsT=ones[:], rhs=vm[:].rearrange("p a b -> p (a b)"), start=True, stop=False)
        nc.tensor.matmul(finf, lhsT=ones[:], rhs=z[:].rearrange("p a b -> p (a b)"), start=False, stop=True)
        nc.scalar.activation(out=row[:], in_=finf, func=ACT.Copy, scale=es[:, 0:1])
        nc.sync.dma_start(out=out_d.rearrange("(o a) b -> o (a b)", o=1), in_=row[0:1, :])
